import numpy as np
import ml_dtypes

BF16 = ml_dtypes.bfloat16


def bf(x):
    return np.asarray(x, np.float32).astype(BF16)


def f32(x):
    return np.asarray(x, np.float32)


def f64(x):
    return np.asarray(x).astype(np.float64)


def striped(idx):
    return np.tile(idx.reshape(-1, 16).T, (8, 1))


S, PF, HP, D, HT, F1, F2, N = 1024, 128, 512, 128, 512, 512, 1024, 2048


def setup_inputs():
    return {
        "person_x": bf(np.random.standard_normal((S, PF))),
        "wp1": bf(np.random.standard_normal((PF, HP)) / np.sqrt(PF)),
        "bp1": f32(0.1 * np.random.standard_normal((HP, 1))),
        "wp2": bf(np.random.standard_normal((HP, D)) / np.sqrt(HP)),
        "bp2": f32(0.1 * np.random.standard_normal((D, 1))),
        "state": bf(np.random.standard_normal((D, N))),
        "t": f32(np.random.uniform(size=(1, N))),
        "wt1": f32(np.random.standard_normal((HT, 1))),
        "bt1": f32(0.1 * np.random.standard_normal((HT, 1))),
        "wt2": bf(np.random.standard_normal((HT, D)) / np.sqrt(HT)),
        "bt2": f32(0.1 * np.random.standard_normal((D, 1))),
        "wf1_s": bf(np.random.standard_normal((D, F1)) / np.sqrt(D + D + D)),
        "wf1_p": bf(np.random.standard_normal((D, F1)) / np.sqrt(D + D + D)),
        "wf1_t": bf(np.random.standard_normal((D, F1)) / np.sqrt(D + D + D)),
        "bias_f1": f32(0.1 * np.random.standard_normal((F1, 1))),
        "wf2": bf(np.random.standard_normal((F1, F2)) / np.sqrt(F1)),
        "bias_f2": f32(0.1 * np.random.standard_normal((F2, 1))),
        "offs": striped(np.random.permutation(np.tile(np.arange(S), 2))[:N]),
    }


def reference(person_x, wp1, bp1, wp2, bp2, state, t, wt1, bt1, wt2, bt2, wf1_s, wf1_p, wf1_t, bias_f1, wf2, bias_f2, offs):
    idx = offs[:16].T.reshape(-1)
    a = np.maximum(f64(wp1).T @ f64(person_x).T + f64(bp1), 0.0)
    pe = f64(wp2).T @ a + f64(bp2)
    u = np.maximum(f64(wt1) * f64(t) + f64(bt1), 0.0)
    te = f64(wt2).T @ u + f64(bt2)
    h = np.maximum(f64(wf1_s).T @ f64(state) + f64(wf1_p).T @ pe[:, idx] + f64(wf1_t).T @ te + f64(bias_f1), 0.0)
    return np.maximum(f64(wf2).T @ h + f64(bias_f2), 0.0)

@@ -1,0 +1,149 @@
+import concourse.mybir as mybir
+from concourse.masks import make_identity
+
+P = 128
+S, PF, HP, D, HT, F1, F2, N = 1024, 128, 512, 128, 512, 512, 1024, 2048
+CH = 512
+FLOPS = 2 * (S * PF * HP + S * HP * D + N * HT * D + 3 * N * D * F1 + N * F1 * F2)
+
+BF16, F32, U16 = mybir.dt.bfloat16, mybir.dt.float32, mybir.dt.uint16
+RELU = mybir.ActivationFunctionType.Relu
+NO_FUNC = mybir.ActivationFunctionType.Identity
+ADD, MAX = mybir.AluOpType.add, mybir.AluOpType.max
+
+
+def tile_manifoldgnnphysicsode_b_kernel(
+    tc, person_x, wp1, bp1, wp2, bp2, state, t, wt1, bt1, wt2, bt2,
+    wf1_s, wf1_p, wf1_t, bias_f1, wf2, bias_f2, offs, out,
+):
+    nc = tc.nc
+
+    def leave_psum(turn, dst, src, bias, relu):
+        if turn % 2 == 0:
+            nc.scalar.activation(dst, src, RELU if relu else NO_FUNC, bias=bias)
+        elif relu:
+            nc.vector.tensor_scalar(dst, src, bias, 0.0, op0=ADD, op1=MAX)
+        else:
+            nc.vector.tensor_scalar_add(dst, src, bias)
+
+    with (
+        tc.tile_pool(name="held", bufs=1) as held,
+        tc.tile_pool(name="hidden", bufs=2) as hidden,
+        tc.tile_pool(name="staged", bufs=6) as staged,
+        tc.psum_pool(name="psum", bufs=4) as psum,
+    ):
+        x_rows = held.tile([P, S // P, PF], BF16, name="x_rows")
+        wp1_sb = held.tile([P, HP], BF16, name="wp1_sb")
+        bp1_sb = held.tile([P, HP // P], F32, name="bp1_sb")
+        wp2_sb = held.tile([P, HP // P, D], BF16, name="wp2_sb")
+        bp2_sb = held.tile([P, 1], F32, name="bp2_sb")
+        offsets = held.tile([P, N // 16], U16, name="offsets")
+        wt1_sb = held.tile([P, HT // P], F32, name="wt1_sb")
+        bt1_sb = held.tile([P, HT // P], F32, name="bt1_sb")
+        wt2_sb = held.tile([P, HT // P, D], BF16, name="wt2_sb")
+        bt2_sb = held.tile([P, 1], F32, name="bt2_sb")
+        wf1_s_sb = held.tile([P, F1], BF16, name="wf1_s_sb")
+        wf1_p_sb = held.tile([P, F1], BF16, name="wf1_p_sb")
+        wf1_t_sb = held.tile([P, F1], BF16, name="wf1_t_sb")
+        bias_f1_sb = held.tile([P, F1 // P], F32, name="bias_f1_sb")
+        wf2_sb = held.tile([P, F1 // P, F2], BF16, name="wf2_sb")
+        bias_f2_sb = held.tile([P, F2 // P], F32, name="bias_f2_sb")
+        state_sb = held.tile([P, N], BF16, name="state_sb")
+        t_all = held.tile([P, N], F32, name="t_all")
+
+        identity = held.tile([P, P], BF16, name="identity")
+        make_identity(nc, identity[:])
+
+        t_row = t.rearrange("o n -> (o n)")
+        nc.sync.dma_start(offsets[:], offs)
+        nc.sync.dma_start(x_rows[:], person_x.rearrange("(b p) k -> p b k", p=P))
+        nc.sync.dma_start(wp1_sb[:], wp1)
+        nc.sync.dma_start(t_all[:, 0:CH], t_row[0:CH].partition_broadcast(P))
+        nc.sync.dma_start(wp2_sb[:], wp2.rearrange("(a p) d -> p a d", p=P))
+        nc.sync.dma_start(wf2_sb[:], wf2.rearrange("(a p) r -> p a r", p=P))
+        nc.scalar.dma_start(wt1_sb[:], wt1.rearrange("(p a) o -> p (a o)", p=P))
+        nc.scalar.dma_start(bt1_sb[:], bt1.rearrange("(p a) o -> p (a o)", p=P))
+        nc.scalar.dma_start(wt2_sb[:], wt2.rearrange("(p a) d -> p a d", p=P))
+        with nc.allow_non_contiguous_dma(reason="biases: one float32 to a partition and block"):
+            nc.scalar.dma_start(bp1_sb[:], bp1.rearrange("(a p) o -> p (a o)", p=P))
+            nc.scalar.dma_start(bp2_sb[:], bp2)
+            nc.scalar.dma_start(bt2_sb[:], bt2)
+            nc.scalar.dma_start(bias_f1_sb[:], bias_f1.rearrange("(a p) o -> p (a o)", p=P))
+            nc.scalar.dma_start(bias_f2_sb[:], bias_f2.rearrange("(a p) o -> p (a o)", p=P))
+        nc.gpsimd.dma_start(state_sb[:, 0:CH], state[:, 0:CH])
+        nc.gpsimd.dma_start(wf1_s_sb[:], wf1_s)
+        nc.gpsimd.dma_start(wf1_t_sb[:], wf1_t)
+        nc.gpsimd.dma_start(wf1_p_sb[:], wf1_p)
+        for c in range(1, N // CH):
+            cols = slice(c * CH, (c + 1) * CH)
+            nc.gpsimd.dma_start(t_all[:, cols], t_row[cols].partition_broadcast(P))
+            nc.gpsimd.dma_start(state_sb[:, cols], state[:, cols])
+
+        x_t = held.tile([P, S], BF16, name="x_t")
+        a_sb = held.tile([P, HP // P, S], BF16, name="a_sb")
+        pe_sb = held.tile([P, S], BF16, name="pe_sb")
+        u_sb = held.tile([P, HT // P, N], BF16, name="u_sb")
+        te_sb = held.tile([P, N], BF16, name="te_sb")
+
+        def time_hidden(c):
+            cols = slice(c * CH, (c + 1) * CH)
+            for a in range(HT // P):
+                nc.scalar.activation(
+                    u_sb[:, a, cols], t_all[:, cols], RELU, bias=bt1_sb[:, a : a + 1], scale=wt1_sb[:, a : a + 1]
+                )
+
+        def time_encoding(c):
+            cols = slice(c * CH, (c + 1) * CH)
+            te_ps = psum.tile([P, CH], F32, name="te_ps", tag="bank")
+            for a in range(HT // P):
+                nc.tensor.matmul(
+                    te_ps[:], wt2_sb[:, a, :], u_sb[:, a, cols], start=(a == 0), stop=(a == HT // P - 1)
+                )
+            leave_psum(c + 1, te_sb[:, cols], te_ps[:], bt2_sb[:, 0:1], relu=False)
+
+        time_hidden(0)
+        for half in range(S // CH):
+            x_t_ps = psum.tile([P, CH], BF16, name="x_t_ps", tag="bank")
+            for q in range(CH // P):
+                nc.tensor.transpose(x_t_ps[:, q * P : (q + 1) * P], x_rows[:, half * (CH // P) + q, :], identity[:])
+            nc.vector.tensor_copy(x_t[:, half * CH : (half + 1) * CH], x_t_ps[:])
+        for half in range(S // CH):
+            cols = slice(half * CH, (half + 1) * CH)
+            for m in range(HP // P):
+                a_ps = psum.tile([P, CH], F32, name="a_ps", tag="bank")
+                nc.tensor.matmul(a_ps[:], wp1_sb[:, m * P : (m + 1) * P], x_t[:, cols], start=True, stop=True)
+                leave_psum(m + 1, a_sb[:, m, cols], a_ps[:], bp1_sb[:, m : m + 1], relu=True)
+        time_encoding(0)
+        for half in range(S // CH):
+            cols = slice(half * CH, (half + 1) * CH)
+            pe_ps = psum.tile([P, CH], F32, name="pe_ps", tag="bank")
+            for m in range(HP // P):
+                nc.tensor.matmul(pe_ps[:], wp2_sb[:, m, :], a_sb[:, m, cols], start=(m == 0), stop=(m == HP // P - 1))
+            leave_psum(half + 1, pe_sb[:, cols], pe_ps[:], bp2_sb[:, 0:1], relu=False)
+
+        for c in range(N // CH):
+            cols = slice(c * CH, (c + 1) * CH)
+            if c + 1 < N // CH:
+                time_hidden(c + 1)
+            h_ps = [psum.tile([P, CH], F32, name="h_ps%d" % m, tag="h_bank") for m in range(F1 // P)]
+            for m in range(F1 // P):
+                nc.tensor.matmul(h_ps[m][:], wf1_s_sb[:, m * P : (m + 1) * P], state_sb[:, cols], start=True, stop=False)
+            for m in range(F1 // P):
+                nc.tensor.matmul(h_ps[m][:], wf1_t_sb[:, m * P : (m + 1) * P], te_sb[:, cols], start=False, stop=False)
+            picked = pe_sb[:].indirect(offsets[:, c * (CH // 16) : (c + 1) * (CH // 16)])
+            for m in range(F1 // P):
+                nc.tensor.matmul(h_ps[m][:], wf1_p_sb[:, m * P : (m + 1) * P], picked, start=False, stop=True)
+            h_sb = hidden.tile([P, F1 // P, CH], BF16, name="h_sb")
+            for m in range(F1 // P):
+                leave_psum(m, h_sb[:, m, :], h_ps[m][:], bias_f1_sb[:, m : m + 1], relu=True)
+            if c + 1 < N // CH:
+                time_encoding(c + 1)
+            for r in range(F2 // P):
+                o_ps = psum.tile([P, CH], F32, name="o_ps", tag="bank")
+                for m in range(F1 // P):
+                    nc.tensor.matmul(
+                        o_ps[:], wf2_sb[:, m, r * P : (r + 1) * P], h_sb[:, m, :], start=(m == 0), stop=(m == F1 // P - 1)
+                    )
+                o_sb = staged.tile([P, CH], F32, name="o_sb")
+                leave_psum(r, o_sb[:], o_ps[:], bias_f2_sb[:, r : r + 1], relu=True)
+                nc.sync.dma_start(out[r * P : (r + 1) * P, cols], o_sb[:])

@@ -55,29 +55,34 @@ def tile_manifoldgnnphysicsode_b_kernel(
         make_identity(nc, identity[:])
 
         t_row = t.rearrange("o n -> (o n)")
-        nc.sync.dma_start(offsets[:], offs)
-        nc.sync.dma_start(x_rows[:], person_x.rearrange("(b p) k -> p b k", p=P))
-        nc.sync.dma_start(wp1_sb[:], wp1)
-        nc.sync.dma_start(t_all[:, 0:CH], t_row[0:CH].partition_broadcast(P))
-        nc.sync.dma_start(wp2_sb[:], wp2.rearrange("(a p) d -> p a d", p=P))
-        nc.sync.dma_start(wf2_sb[:], wf2.rearrange("(a p) r -> p a r", p=P))
-        nc.scalar.dma_start(wt1_sb[:], wt1.rearrange("(p a) o -> p (a o)", p=P))
-        nc.scalar.dma_start(bt1_sb[:], bt1.rearrange("(p a) o -> p (a o)", p=P))
-        nc.scalar.dma_start(wt2_sb[:], wt2.rearrange("(p a) d -> p a d", p=P))
         with nc.allow_non_contiguous_dma(reason="biases: one float32 to a partition and block"):
+            nc.sync.dma_start(x_rows[:], person_x.rearrange("(b p) k -> p b k", p=P))
+            nc.sync.dma_start(wp1_sb[:], wp1)
+            nc.sync.dma_start(t_all[:, 0:CH], t_row[0:CH].partition_broadcast(P))
+            nc.sync.dma_start(wp2_sb[:], wp2.rearrange("(a p) d -> p a d", p=P))
+            nc.sync.dma_start(wf1_t_sb[:], wf1_t)
+            nc.sync.dma_start(wf1_p_sb[:], wf1_p)
+        nc.sync.dma_start(offsets[:], offs)
+        with nc.allow_non_contiguous_dma(reason="biases: one float32 to a partition and block"):
+            nc.sync.dma_start(bp2_sb[:], bp2)
+            nc.sync.dma_start(bt2_sb[:], bt2)
+            nc.sync.dma_start(bias_f1_sb[:], bias_f1.rearrange("(a p) o -> p (a o)", p=P))
+            nc.sync.dma_start(wf2_sb[:], wf2.rearrange("(a p) r -> p a r", p=P))
+            nc.sync.dma_start(bias_f2_sb[:], bias_f2.rearrange("(a p) o -> p (a o)", p=P))
+            nc.scalar.dma_start(wt1_sb[:], wt1.rearrange("(p a) o -> p (a o)", p=P))
+            nc.scalar.dma_start(bt1_sb[:], bt1.rearrange("(p a) o -> p (a o)", p=P))
             nc.scalar.dma_start(bp1_sb[:], bp1.rearrange("(a p) o -> p (a o)", p=P))
-            nc.scalar.dma_start(bp2_sb[:], bp2)
-            nc.scalar.dma_start(bt2_sb[:], bt2)
-            nc.scalar.dma_start(bias_f1_sb[:], bias_f1.rearrange("(a p) o -> p (a o)", p=P))
-            nc.scalar.dma_start(bias_f2_sb[:], bias_f2.rearrange("(a p) o -> p (a o)", p=P))
+            nc.scalar.dma_start(wt2_sb[:], wt2.rearrange("(p a) d -> p a d", p=P))
         nc.gpsimd.dma_start(state_sb[:, 0:CH], state[:, 0:CH])
         nc.gpsimd.dma_start(wf1_s_sb[:], wf1_s)
-        nc.gpsimd.dma_start(wf1_t_sb[:], wf1_t)
-        nc.gpsimd.dma_start(wf1_p_sb[:], wf1_p)
         for c in range(1, N // CH):
             cols = slice(c * CH, (c + 1) * CH)
             nc.gpsimd.dma_start(t_all[:, cols], t_row[cols].partition_broadcast(P))
             nc.gpsimd.dma_start(state_sb[:, cols], state[:, cols])
+
+        warm = held.tile([P, 1], F32, name="warm")
+        nc.vector.memset(warm[:], 0.0)
+        nc.scalar.activation(warm[:], warm[:], RELU)
 
         x_t = held.tile([P, S], BF16, name="x_t")
         a_sb = held.tile([P, HP // P, S], BF16, name="a_sb")
@@ -101,7 +106,6 @@ def tile_manifoldgnnphysicsode_b_kernel(
                 )
             leave_psum(c + 1, te_sb[:, cols], te_ps[:], bt2_sb[:, 0:1], relu=False)
 
-        time_hidden(0)
         for half in range(S // CH):
             x_t_ps = psum.tile([P, CH], BF16, name="x_t_ps", tag="bank")
             for q in range(CH // P):
@@ -112,7 +116,8 @@ def tile_manifoldgnnphysicsode_b_kernel(
             for m in range(HP // P):
                 a_ps = psum.tile([P, CH], F32, name="a_ps", tag="bank")
                 nc.tensor.matmul(a_ps[:], wp1_sb[:, m * P : (m + 1) * P], x_t[:, cols], start=True, stop=True)
-                leave_psum(m + 1, a_sb[:, m, cols], a_ps[:], bp1_sb[:, m : m + 1], relu=True)
+                leave_psum(m, a_sb[:, m, cols], a_ps[:], bp1_sb[:, m : m + 1], relu=True)
+        time_hidden(0)
         time_encoding(0)
         for half in range(S // CH):
             cols = slice(half * CH, (half + 1) * CH)

@@ -55,30 +55,29 @@ def tile_manifoldgnnphysicsode_b_kernel(
         make_identity(nc, identity[:])
 
         t_row = t.rearrange("o n -> (o n)")
+        rest = slice(CH, N)
         with nc.allow_non_contiguous_dma(reason="biases: one float32 to a partition and block"):
+            nc.sync.dma_start(wf1_s_sb[:], wf1_s)
+            nc.scalar.dma_start(state_sb[:, 0:CH], state[:, 0:CH])
+            nc.scalar.dma_start(wt1_sb[:], wt1.rearrange("(p a) o -> p (a o)", p=P))
+            nc.scalar.dma_start(bt1_sb[:], bt1.rearrange("(p a) o -> p (a o)", p=P))
+            nc.sync.dma_start(t_all[:, 0:CH], t_row[0:CH].partition_broadcast(P))
             nc.sync.dma_start(x_rows[:], person_x.rearrange("(b p) k -> p b k", p=P))
             nc.sync.dma_start(wp1_sb[:], wp1)
-            nc.sync.dma_start(t_all[:, 0:CH], t_row[0:CH].partition_broadcast(P))
+            nc.scalar.dma_start(bp1_sb[:], bp1.rearrange("(a p) o -> p (a o)", p=P))
+            nc.sync.dma_start(wt2_sb[:], wt2.rearrange("(p a) d -> p a d", p=P))
             nc.sync.dma_start(wp2_sb[:], wp2.rearrange("(a p) d -> p a d", p=P))
+            nc.sync.dma_start(bt2_sb[:], bt2)
+            nc.sync.dma_start(bp2_sb[:], bp2)
             nc.sync.dma_start(wf1_t_sb[:], wf1_t)
             nc.sync.dma_start(wf1_p_sb[:], wf1_p)
         nc.sync.dma_start(offsets[:], offs)
         with nc.allow_non_contiguous_dma(reason="biases: one float32 to a partition and block"):
-            nc.sync.dma_start(bp2_sb[:], bp2)
-            nc.sync.dma_start(bt2_sb[:], bt2)
             nc.sync.dma_start(bias_f1_sb[:], bias_f1.rearrange("(a p) o -> p (a o)", p=P))
             nc.sync.dma_start(wf2_sb[:], wf2.rearrange("(a p) r -> p a r", p=P))
             nc.sync.dma_start(bias_f2_sb[:], bias_f2.rearrange("(a p) o -> p (a o)", p=P))
-            nc.scalar.dma_start(wt1_sb[:], wt1.rearrange("(p a) o -> p (a o)", p=P))
-            nc.scalar.dma_start(bt1_sb[:], bt1.rearrange("(p a) o -> p (a o)", p=P))
-            nc.scalar.dma_start(bp1_sb[:], bp1.rearrange("(a p) o -> p (a o)", p=P))
-            nc.scalar.dma_start(wt2_sb[:], wt2.rearrange("(p a) d -> p a d", p=P))
-        nc.gpsimd.dma_start(state_sb[:, 0:CH], state[:, 0:CH])
-        nc.gpsimd.dma_start(wf1_s_sb[:], wf1_s)
-        for c in range(1, N // CH):
-            cols = slice(c * CH, (c + 1) * CH)
-            nc.gpsimd.dma_start(t_all[:, cols], t_row[cols].partition_broadcast(P))
-            nc.gpsimd.dma_start(state_sb[:, cols], state[:, cols])
+        nc.sync.dma_start(state_sb[:, rest], state[:, rest])
+        nc.sync.dma_start(t_all[:, rest], t_row[rest].partition_broadcast(P))
 
         warm = held.tile([P, 1], F32, name="warm")
         nc.vector.memset(warm[:], 0.0)
@@ -106,6 +105,16 @@ def tile_manifoldgnnphysicsode_b_kernel(
                 )
             leave_psum(c + 1, te_sb[:, cols], te_ps[:], bt2_sb[:, 0:1], relu=False)
 
+        def open_first_layer(c):
+            cols = slice(c * CH, (c + 1) * CH)
+            h_ps = [psum.tile([P, CH], F32, name="h_ps%d" % m, tag="h_bank") for m in range(F1 // P)]
+            for m in range(F1 // P):
+                nc.tensor.matmul(h_ps[m][:], wf1_s_sb[:, m * P : (m + 1) * P], state_sb[:, cols], start=True, stop=False)
+            return h_ps
+
+        h_ps = open_first_layer(0)
+        time_hidden(0)
+
         for half in range(S // CH):
             x_t_ps = psum.tile([P, CH], BF16, name="x_t_ps", tag="bank")
             for q in range(CH // P):
@@ -117,7 +126,6 @@ def tile_manifoldgnnphysicsode_b_kernel(
                 a_ps = psum.tile([P, CH], F32, name="a_ps", tag="bank")
                 nc.tensor.matmul(a_ps[:], wp1_sb[:, m * P : (m + 1) * P], x_t[:, cols], start=True, stop=True)
                 leave_psum(m, a_sb[:, m, cols], a_ps[:], bp1_sb[:, m : m + 1], relu=True)
-        time_hidden(0)
         time_encoding(0)
         for half in range(S // CH):
             cols = slice(half * CH, (half + 1) * CH)
@@ -130,9 +138,6 @@ def tile_manifoldgnnphysicsode_b_kernel(
             cols = slice(c * CH, (c + 1) * CH)
             if c + 1 < N // CH:
                 time_hidden(c + 1)
-            h_ps = [psum.tile([P, CH], F32, name="h_ps%d" % m, tag="h_bank") for m in range(F1 // P)]
-            for m in range(F1 // P):
-                nc.tensor.matmul(h_ps[m][:], wf1_s_sb[:, m * P : (m + 1) * P], state_sb[:, cols], start=True, stop=False)
             for m in range(F1 // P):
                 nc.tensor.matmul(h_ps[m][:], wf1_t_sb[:, m * P : (m + 1) * P], te_sb[:, cols], start=False, stop=False)
             picked = pe_sb[:].indirect(offsets[:, c * (CH // 16) : (c + 1) * (CH // 16)])
@@ -143,6 +148,7 @@ def tile_manifoldgnnphysicsode_b_kernel(
                 leave_psum(m, h_sb[:, m, :], h_ps[m][:], bias_f1_sb[:, m : m + 1], relu=True)
             if c + 1 < N // CH:
                 time_encoding(c + 1)
+                h_ps = open_first_layer(c + 1)
             for r in range(F2 // P):
                 o_ps = psum.tile([P, CH], F32, name="o_ps", tag="bank")
                 for m in range(F1 // P):

@@ -150,11 +150,16 @@ def tile_manifoldgnnphysicsode_b_kernel(
                 time_encoding(c + 1)
                 h_ps = open_first_layer(c + 1)
             for r in range(F2 // P):
-                o_ps = psum.tile([P, CH], F32, name="o_ps", tag="bank")
-                for m in range(F1 // P):
-                    nc.tensor.matmul(
-                        o_ps[:], wf2_sb[:, m, r * P : (r + 1) * P], h_sb[:, m, :], start=(m == 0), stop=(m == F1 // P - 1)
-                    )
-                o_sb = staged.tile([P, CH], F32, name="o_sb")
-                leave_psum(r, o_sb[:], o_ps[:], bias_f2_sb[:, r : r + 1], relu=True)
-                nc.sync.dma_start(out[r * P : (r + 1) * P, cols], o_sb[:])
+                last_block = c == N // CH - 1 and r == F2 // P - 1
+                width = CH // 2 if last_block else CH
+                for piece in range(CH // width):
+                    lo = piece * width
+                    o_ps = psum.tile([P, width], F32, name="o_ps", tag="bank")
+                    for m in range(F1 // P):
+                        nc.tensor.matmul(
+                            o_ps[:], wf2_sb[:, m, r * P : (r + 1) * P], h_sb[:, m, lo : lo + width],
+                            start=(m == 0), stop=(m == F1 // P - 1),
+                        )
+                    o_sb = staged.tile([P, width], F32, name="o_sb")
+                    leave_psum(r + piece, o_sb[:], o_ps[:], bias_f2_sb[:, r : r + 1], relu=True)
+                    nc.sync.dma_start(out[r * P : (r + 1) * P, c * CH + lo : c * CH + lo + width], o_sb[:])

@@ -61,8 +61,8 @@ def tile_manifoldgnnphysicsode_b_kernel(
             nc.scalar.dma_start(state_sb[:, 0:CH], state[:, 0:CH])
             nc.scalar.dma_start(wt1_sb[:], wt1.rearrange("(p a) o -> p (a o)", p=P))
             nc.scalar.dma_start(bt1_sb[:], bt1.rearrange("(p a) o -> p (a o)", p=P))
-            nc.sync.dma_start(t_all[:, 0:CH], t_row[0:CH].partition_broadcast(P))
             nc.sync.dma_start(x_rows[:], person_x.rearrange("(b p) k -> p b k", p=P))
+            nc.sync.dma_start(t_all[:, 0:CH], t_row[0:CH].partition_broadcast(P))
             nc.sync.dma_start(wp1_sb[:], wp1)
             nc.scalar.dma_start(bp1_sb[:], bp1.rearrange("(a p) o -> p (a o)", p=P))
             nc.sync.dma_start(wt2_sb[:], wt2.rearrange("(p a) d -> p a d", p=P))
@@ -112,14 +112,14 @@ def tile_manifoldgnnphysicsode_b_kernel(
                 nc.tensor.matmul(h_ps[m][:], wf1_s_sb[:, m * P : (m + 1) * P], state_sb[:, cols], start=True, stop=False)
             return h_ps
 
-        h_ps = open_first_layer(0)
-        time_hidden(0)
-
         for half in range(S // CH):
             x_t_ps = psum.tile([P, CH], BF16, name="x_t_ps", tag="bank")
             for q in range(CH // P):
                 nc.tensor.transpose(x_t_ps[:, q * P : (q + 1) * P], x_rows[:, half * (CH // P) + q, :], identity[:])
             nc.vector.tensor_copy(x_t[:, half * CH : (half + 1) * CH], x_t_ps[:])
+        h_ps = open_first_layer(0)
+        time_hidden(0)
+
         for half in range(S // CH):
             cols = slice(half * CH, (half + 1) * CH)
             for m in range(HP // P):
@@ -151,7 +151,7 @@ def tile_manifoldgnnphysicsode_b_kernel(
                 h_ps = open_first_layer(c + 1)
             for r in range(F2 // P):
                 last_block = c == N // CH - 1 and r == F2 // P - 1
-                width = CH // 2 if last_block else CH
+                width = CH // 4 if last_block else CH
                 for piece in range(CH // width):
                     lo = piece * width
                     o_ps = psum.tile([P, width], F32, name="o_ps", tag="bank")

@@ -162,4 +162,5 @@ def tile_manifoldgnnphysicsode_b_kernel(
                         )
                     o_sb = staged.tile([P, width], F32, name="o_sb")
                     leave_psum(r + piece, o_sb[:], o_ps[:], bias_f2_sb[:, r : r + 1], relu=True)
-                    nc.sync.dma_start(out[r * P : (r + 1) * P, c * CH + lo : c * CH + lo + width], o_sb[:])
+                    store_queue = nc.scalar if (r + piece) % 2 == 0 else nc.sync
+                    store_queue.dma_start(out[r * P : (r + 1) * P, c * CH + lo : c * CH + lo + width], o_sb[:])

@@ -57,8 +57,9 @@ def tile_manifoldgnnphysicsode_b_kernel(
         t_row = t.rearrange("o n -> (o n)")
         rest = slice(CH, N)
         with nc.allow_non_contiguous_dma(reason="biases: one float32 to a partition and block"):
-            nc.sync.dma_start(wf1_s_sb[:], wf1_s)
+            nc.sync.dma_start(wf1_s_sb[:, 0:P], wf1_s[:, 0:P])
             nc.scalar.dma_start(state_sb[:, 0:CH], state[:, 0:CH])
+            nc.sync.dma_start(wf1_s_sb[:, P:F1], wf1_s[:, P:F1])
             nc.scalar.dma_start(wt1_sb[:], wt1.rearrange("(p a) o -> p (a o)", p=P))
             nc.scalar.dma_start(bt1_sb[:], bt1.rearrange("(p a) o -> p (a o)", p=P))
             nc.sync.dma_start(x_rows[:], person_x.rearrange("(b p) k -> p b k", p=P))
@@ -75,9 +76,10 @@ def tile_manifoldgnnphysicsode_b_kernel(
         with nc.allow_non_contiguous_dma(reason="biases: one float32 to a partition and block"):
             nc.sync.dma_start(bias_f1_sb[:], bias_f1.rearrange("(a p) o -> p (a o)", p=P))
             nc.sync.dma_start(wf2_sb[:], wf2.rearrange("(a p) r -> p a r", p=P))
+            nc.sync.dma_start(t_all[:, CH : 2 * CH], t_row[CH : 2 * CH].partition_broadcast(P))
             nc.sync.dma_start(bias_f2_sb[:], bias_f2.rearrange("(a p) o -> p (a o)", p=P))
         nc.sync.dma_start(state_sb[:, rest], state[:, rest])
-        nc.sync.dma_start(t_all[:, rest], t_row[rest].partition_broadcast(P))
+        nc.sync.dma_start(t_all[:, 2 * CH : N], t_row[2 * CH : N].partition_broadcast(P))
 
         warm = held.tile([P, 1], F32, name="warm")
         nc.vector.memset(warm[:], 0.0)
@@ -103,7 +105,7 @@ def tile_manifoldgnnphysicsode_b_kernel(
                 nc.tensor.matmul(
                     te_ps[:], wt2_sb[:, a, :], u_sb[:, a, cols], start=(a == 0), stop=(a == HT // P - 1)
                 )
-            leave_psum(c + 1, te_sb[:, cols], te_ps[:], bt2_sb[:, 0:1], relu=False)
+            leave_psum(1, te_sb[:, cols], te_ps[:], bt2_sb[:, 0:1], relu=False)
 
         def open_first_layer(c):
             cols = slice(c * CH, (c + 1) * CH)
@@ -132,7 +134,7 @@ def tile_manifoldgnnphysicsode_b_kernel(
             pe_ps = psum.tile([P, CH], F32, name="pe_ps", tag="bank")
             for m in range(HP // P):
                 nc.tensor.matmul(pe_ps[:], wp2_sb[:, m, :], a_sb[:, m, cols], start=(m == 0), stop=(m == HP // P - 1))
-            leave_psum(half + 1, pe_sb[:, cols], pe_ps[:], bp2_sb[:, 0:1], relu=False)
+            leave_psum(1, pe_sb[:, cols], pe_ps[:], bp2_sb[:, 0:1], relu=False)
 
         for c in range(N // CH):
             cols = slice(c * CH, (c + 1) * CH)
@@ -145,7 +147,7 @@ def tile_manifoldgnnphysicsode_b_kernel(
                 nc.tensor.matmul(h_ps[m][:], wf1_p_sb[:, m * P : (m + 1) * P], picked, start=False, stop=True)
             h_sb = hidden.tile([P, F1 // P, CH], BF16, name="h_sb")
             for m in range(F1 // P):
-                leave_psum(m, h_sb[:, m, :], h_ps[m][:], bias_f1_sb[:, m : m + 1], relu=True)
+                leave_psum(1, h_sb[:, m, :], h_ps[m][:], bias_f1_sb[:, m : m + 1], relu=True)
             if c + 1 < N // CH:
                 time_encoding(c + 1)
                 h_ps = open_first_layer(c + 1)

@@ -127,7 +127,8 @@ def tile_manifoldgnnphysicsode_b_kernel(
             for m in range(HP // P):
                 a_ps = psum.tile([P, CH], F32, name="a_ps", tag="bank")
                 nc.tensor.matmul(a_ps[:], wp1_sb[:, m * P : (m + 1) * P], x_t[:, cols], start=True, stop=True)
-                leave_psum(m, a_sb[:, m, cols], a_ps[:], bp1_sb[:, m : m + 1], relu=True)
+                bank = half * (HP // P) + m
+                leave_psum(1 if bank < 3 else bank + 1, a_sb[:, m, cols], a_ps[:], bp1_sb[:, m : m + 1], relu=True)
         time_encoding(0)
         for half in range(S // CH):
             cols = slice(half * CH, (half + 1) * CH)

@@ -165,5 +165,11 @@ def tile_manifoldgnnphysicsode_b_kernel(
                         )
                     o_sb = staged.tile([P, width], F32, name="o_sb")
                     leave_psum(r + piece, o_sb[:], o_ps[:], bias_f2_sb[:, r : r + 1], relu=True)
-                    store_queue = nc.scalar if (r + piece) % 2 == 0 else nc.sync
-                    store_queue.dma_start(out[r * P : (r + 1) * P, c * CH + lo : c * CH + lo + width], o_sb[:])
+                    rows = out[r * P : (r + 1) * P, :]
+                    first = c * CH + lo
+                    if last_block:
+                        store_queue = nc.scalar if (r + piece) % 2 == 0 else nc.sync
+                        store_queue.dma_start(rows[:, first : first + width], o_sb[:])
+                    else:
+                        nc.sync.dma_start(rows[:, first : first + CH // 2], o_sb[:, 0 : CH // 2])
+                        nc.scalar.dma_start(rows[:, first + CH // 2 : first + CH], o_sb[:, CH // 2 : CH])

@@ -28,6 +28,7 @@ def tile_manifoldgnnphysicsode_b_kernel(
 
     with (
         tc.tile_pool(name="held", bufs=1) as held,
+        tc.tile_pool(name="takeover", bufs=1) as takeover,
         tc.tile_pool(name="hidden", bufs=2) as hidden,
         tc.tile_pool(name="staged", bufs=6) as staged,
         tc.psum_pool(name="psum", bufs=4) as psum,
@@ -85,25 +86,29 @@ def tile_manifoldgnnphysicsode_b_kernel(
         nc.vector.memset(warm[:], 0.0)
         nc.scalar.activation(warm[:], warm[:], RELU)
 
-        x_t = held.tile([P, S], BF16, name="x_t")
+        x_t = takeover.tile([P, S], BF16, name="x_t", tag="x_t_then_u")
         a_sb = held.tile([P, HP // P, S], BF16, name="a_sb")
         pe_sb = held.tile([P, S], BF16, name="pe_sb")
-        u_sb = held.tile([P, HT // P, N], BF16, name="u_sb")
         te_sb = held.tile([P, N], BF16, name="te_sb")
 
         def time_hidden(c):
             cols = slice(c * CH, (c + 1) * CH)
+            if c == 0:
+                u_sb = takeover.tile([P, HT // P, CH], BF16, name="u_first", tag="x_t_then_u")
+            else:
+                u_sb = hidden.tile([P, HT // P, CH], BF16, name="u_sb")
             for a in range(HT // P):
                 nc.scalar.activation(
-                    u_sb[:, a, cols], t_all[:, cols], RELU, bias=bt1_sb[:, a : a + 1], scale=wt1_sb[:, a : a + 1]
+                    u_sb[:, a, :], t_all[:, cols], RELU, bias=bt1_sb[:, a : a + 1], scale=wt1_sb[:, a : a + 1]
                 )
+            return u_sb
 
-        def time_encoding(c):
+        def time_encoding(c, u_sb):
             cols = slice(c * CH, (c + 1) * CH)
             te_ps = psum.tile([P, CH], F32, name="te_ps", tag="bank")
             for a in range(HT // P):
                 nc.tensor.matmul(
-                    te_ps[:], wt2_sb[:, a, :], u_sb[:, a, cols], start=(a == 0), stop=(a == HT // P - 1)
+                    te_ps[:], wt2_sb[:, a, :], u_sb[:, a, :], start=(a == 0), stop=(a == HT // P - 1)
                 )
             leave_psum(1, te_sb[:, cols], te_ps[:], bt2_sb[:, 0:1], relu=False)
 
@@ -114,13 +119,22 @@ def tile_manifoldgnnphysicsode_b_kernel(
                 nc.tensor.matmul(h_ps[m][:], wf1_s_sb[:, m * P : (m + 1) * P], state_sb[:, cols], start=True, stop=False)
             return h_ps
 
+        def time_product(c, h_ps, closes):
+            cols = slice(c * CH, (c + 1) * CH)
+            for m in range(F1 // P):
+                nc.tensor.matmul(h_ps[m][:], wf1_t_sb[:, m * P : (m + 1) * P], te_sb[:, cols], start=False, stop=closes)
+
+        def look_up(c, h_ps, closes):
+            picked = pe_sb[:].indirect(offsets[:, c * (CH // 16) : (c + 1) * (CH // 16)])
+            for m in range(F1 // P):
+                nc.tensor.matmul(h_ps[m][:], wf1_p_sb[:, m * P : (m + 1) * P], picked, start=False, stop=closes)
+
         for half in range(S // CH):
             x_t_ps = psum.tile([P, CH], BF16, name="x_t_ps", tag="bank")
             for q in range(CH // P):
                 nc.tensor.transpose(x_t_ps[:, q * P : (q + 1) * P], x_rows[:, half * (CH // P) + q, :], identity[:])
             nc.vector.tensor_copy(x_t[:, half * CH : (half + 1) * CH], x_t_ps[:])
         h_ps = open_first_layer(0)
-        time_hidden(0)
 
         for half in range(S // CH):
             cols = slice(half * CH, (half + 1) * CH)
@@ -128,29 +142,30 @@ def tile_manifoldgnnphysicsode_b_kernel(
                 a_ps = psum.tile([P, CH], F32, name="a_ps", tag="bank")
                 nc.tensor.matmul(a_ps[:], wp1_sb[:, m * P : (m + 1) * P], x_t[:, cols], start=True, stop=True)
                 bank = half * (HP // P) + m
-                leave_psum(1 if bank < 3 else bank + 1, a_sb[:, m, cols], a_ps[:], bp1_sb[:, m : m + 1], relu=True)
-        time_encoding(0)
+                leave_psum(1 if bank == S // CH * (HP // P) - 1 else bank + 1, a_sb[:, m, cols], a_ps[:], bp1_sb[:, m : m + 1], relu=True)
         for half in range(S // CH):
             cols = slice(half * CH, (half + 1) * CH)
             pe_ps = psum.tile([P, CH], F32, name="pe_ps", tag="bank")
             for m in range(HP // P):
                 nc.tensor.matmul(pe_ps[:], wp2_sb[:, m, :], a_sb[:, m, cols], start=(m == 0), stop=(m == HP // P - 1))
             leave_psum(1, pe_sb[:, cols], pe_ps[:], bp2_sb[:, 0:1], relu=False)
+        time_encoding(0, time_hidden(0))
 
         for c in range(N // CH):
             cols = slice(c * CH, (c + 1) * CH)
             if c + 1 < N // CH:
-                time_hidden(c + 1)
-            for m in range(F1 // P):
-                nc.tensor.matmul(h_ps[m][:], wf1_t_sb[:, m * P : (m + 1) * P], te_sb[:, cols], start=False, stop=False)
-            picked = pe_sb[:].indirect(offsets[:, c * (CH // 16) : (c + 1) * (CH // 16)])
-            for m in range(F1 // P):
-                nc.tensor.matmul(h_ps[m][:], wf1_p_sb[:, m * P : (m + 1) * P], picked, start=False, stop=True)
+                u_next = time_hidden(c + 1)
+            if c == 0:
+                look_up(c, h_ps, closes=False)
+                time_product(c, h_ps, closes=True)
+            else:
+                time_product(c, h_ps, closes=False)
+                look_up(c, h_ps, closes=True)
             h_sb = hidden.tile([P, F1 // P, CH], BF16, name="h_sb")
             for m in range(F1 // P):
                 leave_psum(1, h_sb[:, m, :], h_ps[m][:], bias_f1_sb[:, m : m + 1], relu=True)
             if c + 1 < N // CH:
-                time_encoding(c + 1)
+                time_encoding(c + 1, u_next)
                 h_ps = open_first_layer(c + 1)
             for r in range(F2 // P):
                 last_block = c == N // CH - 1 and r == F2 // P - 1

@@ -64,17 +64,17 @@ def tile_manifoldgnnphysicsode_b_kernel(
             nc.scalar.dma_start(wt1_sb[:], wt1.rearrange("(p a) o -> p (a o)", p=P))
             nc.scalar.dma_start(bt1_sb[:], bt1.rearrange("(p a) o -> p (a o)", p=P))
             nc.sync.dma_start(x_rows[:], person_x.rearrange("(b p) k -> p b k", p=P))
-            nc.sync.dma_start(t_all[:, 0:CH], t_row[0:CH].partition_broadcast(P))
             nc.sync.dma_start(wp1_sb[:], wp1)
-            nc.scalar.dma_start(bp1_sb[:], bp1.rearrange("(a p) o -> p (a o)", p=P))
-            nc.sync.dma_start(wt2_sb[:], wt2.rearrange("(p a) d -> p a d", p=P))
             nc.sync.dma_start(wp2_sb[:], wp2.rearrange("(a p) d -> p a d", p=P))
-            nc.sync.dma_start(bt2_sb[:], bt2)
+            nc.scalar.dma_start(bp1_sb[:], bp1.rearrange("(a p) o -> p (a o)", p=P))
             nc.sync.dma_start(bp2_sb[:], bp2)
-            nc.sync.dma_start(wf1_t_sb[:], wf1_t)
+            nc.sync.dma_start(t_all[:, 0:CH], t_row[0:CH].partition_broadcast(P))
+            nc.sync.dma_start(wt2_sb[:], wt2.rearrange("(p a) d -> p a d", p=P))
             nc.sync.dma_start(wf1_p_sb[:], wf1_p)
         nc.sync.dma_start(offsets[:], offs)
         with nc.allow_non_contiguous_dma(reason="biases: one float32 to a partition and block"):
+            nc.sync.dma_start(bt2_sb[:], bt2)
+            nc.sync.dma_start(wf1_t_sb[:], wf1_t)
             nc.sync.dma_start(bias_f1_sb[:], bias_f1.rearrange("(a p) o -> p (a o)", p=P))
             nc.sync.dma_start(wf2_sb[:], wf2.rearrange("(a p) r -> p a r", p=P))
             nc.sync.dma_start(t_all[:, CH : 2 * CH], t_row[CH : 2 * CH].partition_broadcast(P))
@@ -112,11 +112,11 @@ def tile_manifoldgnnphysicsode_b_kernel(
                 )
             leave_psum(1, te_sb[:, cols], te_ps[:], bt2_sb[:, 0:1], relu=False)
 
-        def open_first_layer(c):
+        def open_first_layer(c, blocks):
             cols = slice(c * CH, (c + 1) * CH)
-            h_ps = [psum.tile([P, CH], F32, name="h_ps%d" % m, tag="h_bank") for m in range(F1 // P)]
-            for m in range(F1 // P):
-                nc.tensor.matmul(h_ps[m][:], wf1_s_sb[:, m * P : (m + 1) * P], state_sb[:, cols], start=True, stop=False)
+            h_ps = [psum.tile([P, CH], F32, name="h_ps%d" % m, tag="h_bank") for m in blocks]
+            for bank, m in zip(h_ps, blocks):
+                nc.tensor.matmul(bank[:], wf1_s_sb[:, m * P : (m + 1) * P], state_sb[:, cols], start=True, stop=False)
             return h_ps
 
         def time_product(c, h_ps, closes):
@@ -129,12 +129,13 @@ def tile_manifoldgnnphysicsode_b_kernel(
             for m in range(F1 // P):
                 nc.tensor.matmul(h_ps[m][:], wf1_p_sb[:, m * P : (m + 1) * P], picked, start=False, stop=closes)
 
+        h_ps = open_first_layer(0, range(F1 // P - 1))
         for half in range(S // CH):
-            x_t_ps = psum.tile([P, CH], BF16, name="x_t_ps", tag="bank")
+            x_t_ps = psum.tile([P, CH], BF16, name="x_t_ps", tag="h_bank" if half == 0 else "bank")
             for q in range(CH // P):
                 nc.tensor.transpose(x_t_ps[:, q * P : (q + 1) * P], x_rows[:, half * (CH // P) + q, :], identity[:])
             nc.vector.tensor_copy(x_t[:, half * CH : (half + 1) * CH], x_t_ps[:])
-        h_ps = open_first_layer(0)
+        h_ps = h_ps + open_first_layer(0, [F1 // P - 1])
 
         for half in range(S // CH):
             cols = slice(half * CH, (half + 1) * CH)
@@ -166,7 +167,7 @@ def tile_manifoldgnnphysicsode_b_kernel(
                 leave_psum(1, h_sb[:, m, :], h_ps[m][:], bias_f1_sb[:, m : m + 1], relu=True)
             if c + 1 < N // CH:
                 time_encoding(c + 1, u_next)
-                h_ps = open_first_layer(c + 1)
+                h_ps = open_first_layer(c + 1, range(F1 // P))
             for r in range(F2 // P):
                 last_block = c == N // CH - 1 and r == F2 // P - 1
                 width = CH // 4 if last_block else CH

@@ -76,8 +76,8 @@ def tile_manifoldgnnphysicsode_b_kernel(
             nc.sync.dma_start(bt2_sb[:], bt2)
             nc.sync.dma_start(wf1_t_sb[:], wf1_t)
             nc.sync.dma_start(bias_f1_sb[:], bias_f1.rearrange("(a p) o -> p (a o)", p=P))
-            nc.sync.dma_start(wf2_sb[:], wf2.rearrange("(a p) r -> p a r", p=P))
             nc.sync.dma_start(t_all[:, CH : 2 * CH], t_row[CH : 2 * CH].partition_broadcast(P))
+            nc.sync.dma_start(wf2_sb[:], wf2.rearrange("(a p) r -> p a r", p=P))
             nc.sync.dma_start(bias_f2_sb[:], bias_f2.rearrange("(a p) o -> p (a o)", p=P))
         nc.sync.dma_start(state_sb[:, rest], state[:, rest])
         nc.sync.dma_start(t_all[:, 2 * CH : N], t_row[2 * CH : N].partition_broadcast(P))
@@ -93,10 +93,7 @@ def tile_manifoldgnnphysicsode_b_kernel(
 
         def time_hidden(c):
             cols = slice(c * CH, (c + 1) * CH)
-            if c == 0:
-                u_sb = takeover.tile([P, HT // P, CH], BF16, name="u_first", tag="x_t_then_u")
-            else:
-                u_sb = hidden.tile([P, HT // P, CH], BF16, name="u_sb")
+            u_sb = takeover.tile([P, HT // P, CH], BF16, name="u_sb", tag="x_t_then_u")
             for a in range(HT // P):
                 nc.scalar.activation(
                     u_sb[:, a, :], t_all[:, cols], RELU, bias=bt1_sb[:, a : a + 1], scale=wt1_sb[:, a : a + 1]
@@ -112,11 +109,11 @@ def tile_manifoldgnnphysicsode_b_kernel(
                 )
             leave_psum(1, te_sb[:, cols], te_ps[:], bt2_sb[:, 0:1], relu=False)
 
-        def open_first_layer(c, blocks):
+        def open_first_layer(c):
             cols = slice(c * CH, (c + 1) * CH)
-            h_ps = [psum.tile([P, CH], F32, name="h_ps%d" % m, tag="h_bank") for m in blocks]
-            for bank, m in zip(h_ps, blocks):
-                nc.tensor.matmul(bank[:], wf1_s_sb[:, m * P : (m + 1) * P], state_sb[:, cols], start=True, stop=False)
+            h_ps = [psum.tile([P, CH], F32, name="h_ps%d" % m, tag="h_bank") for m in range(F1 // P)]
+            for m in range(F1 // P):
+                nc.tensor.matmul(h_ps[m][:], wf1_s_sb[:, m * P : (m + 1) * P], state_sb[:, cols], start=True, stop=False)
             return h_ps
 
         def time_product(c, h_ps, closes):
@@ -129,13 +126,12 @@ def tile_manifoldgnnphysicsode_b_kernel(
             for m in range(F1 // P):
                 nc.tensor.matmul(h_ps[m][:], wf1_p_sb[:, m * P : (m + 1) * P], picked, start=False, stop=closes)
 
-        h_ps = open_first_layer(0, range(F1 // P - 1))
         for half in range(S // CH):
-            x_t_ps = psum.tile([P, CH], BF16, name="x_t_ps", tag="h_bank" if half == 0 else "bank")
+            x_t_ps = psum.tile([P, CH], BF16, name="x_t_ps", tag="bank")
             for q in range(CH // P):
                 nc.tensor.transpose(x_t_ps[:, q * P : (q + 1) * P], x_rows[:, half * (CH // P) + q, :], identity[:])
             nc.vector.tensor_copy(x_t[:, half * CH : (half + 1) * CH], x_t_ps[:])
-        h_ps = h_ps + open_first_layer(0, [F1 // P - 1])
+        h_ps = open_first_layer(0)
 
         for half in range(S // CH):
             cols = slice(half * CH, (half + 1) * CH)
@@ -167,7 +163,7 @@ def tile_manifoldgnnphysicsode_b_kernel(
                 leave_psum(1, h_sb[:, m, :], h_ps[m][:], bias_f1_sb[:, m : m + 1], relu=True)
             if c + 1 < N // CH:
                 time_encoding(c + 1, u_next)
-                h_ps = open_first_layer(c + 1, range(F1 // P))
+                h_ps = open_first_layer(c + 1)
             for r in range(F2 // P):
                 last_block = c == N // CH - 1 and r == F2 // P - 1
                 width = CH // 4 if last_block else CH

import concourse.mybir as mybir
from concourse.masks import make_identity

P = 128
S, PF, HP, D, HT, F1, F2, N = 1024, 128, 512, 128, 512, 512, 1024, 2048
CH = 512
FLOPS = 2 * (S * PF * HP + S * HP * D + N * HT * D + 3 * N * D * F1 + N * F1 * F2)

BF16, F32, U16 = mybir.dt.bfloat16, mybir.dt.float32, mybir.dt.uint16
RELU = mybir.ActivationFunctionType.Relu
NO_FUNC = mybir.ActivationFunctionType.Identity
ADD, MAX = mybir.AluOpType.add, mybir.AluOpType.max


def tile_manifoldgnnphysicsode_b_kernel(
    tc, person_x, wp1, bp1, wp2, bp2, state, t, wt1, bt1, wt2, bt2,
    wf1_s, wf1_p, wf1_t, bias_f1, wf2, bias_f2, offs, out,
):
    nc = tc.nc

    def leave_psum(turn, dst, src, bias, relu):
        if turn % 2 == 0:
            nc.scalar.activation(dst, src, RELU if relu else NO_FUNC, bias=bias)
        elif relu:
            nc.vector.tensor_scalar(dst, src, bias, 0.0, op0=ADD, op1=MAX)
        else:
            nc.vector.tensor_scalar_add(dst, src, bias)

    with (
        tc.tile_pool(name="held", bufs=1) as held,
        tc.tile_pool(name="takeover", bufs=1) as takeover,
        tc.tile_pool(name="hidden", bufs=2) as hidden,
        tc.tile_pool(name="staged", bufs=6) as staged,
        tc.psum_pool(name="psum", bufs=4) as psum,
    ):
        x_rows = held.tile([P, S // P, PF], BF16, name="x_rows")
        wp1_sb = held.tile([P, HP], BF16, name="wp1_sb")
        bp1_sb = held.tile([P, HP // P], F32, name="bp1_sb")
        wp2_sb = held.tile([P, HP // P, D], BF16, name="wp2_sb")
        bp2_sb = held.tile([P, 1], F32, name="bp2_sb")
        offsets = held.tile([P, N // 16], U16, name="offsets")
        wt1_sb = held.tile([P, HT // P], F32, name="wt1_sb")
        bt1_sb = held.tile([P, HT // P], F32, name="bt1_sb")
        wt2_sb = held.tile([P, HT // P, D], BF16, name="wt2_sb")
        bt2_sb = held.tile([P, 1], F32, name="bt2_sb")
        wf1_s_sb = held.tile([P, F1], BF16, name="wf1_s_sb")
        wf1_p_sb = held.tile([P, F1], BF16, name="wf1_p_sb")
        wf1_t_sb = held.tile([P, F1], BF16, name="wf1_t_sb")
        bias_f1_sb = held.tile([P, F1 // P], F32, name="bias_f1_sb")
        wf2_sb = held.tile([P, F1 // P, F2], BF16, name="wf2_sb")
        bias_f2_sb = held.tile([P, F2 // P], F32, name="bias_f2_sb")
        state_sb = held.tile([P, N], BF16, name="state_sb")
        t_all = held.tile([P, N], F32, name="t_all")

        identity = held.tile([P, P], BF16, name="identity")
        make_identity(nc, identity[:])

        t_row = t.rearrange("o n -> (o n)")
        rest = slice(CH, N)
        with nc.allow_non_contiguous_dma(reason="biases: one float32 to a partition and block"):
            nc.sync.dma_start(wf1_s_sb[:, 0:P], wf1_s[:, 0:P])
            nc.scalar.dma_start(state_sb[:, 0:CH], state[:, 0:CH])
            nc.sync.dma_start(wf1_s_sb[:, P:F1], wf1_s[:, P:F1])
            nc.scalar.dma_start(wt1_sb[:], wt1.rearrange("(p a) o -> p (a o)", p=P))
            nc.scalar.dma_start(bt1_sb[:], bt1.rearrange("(p a) o -> p (a o)", p=P))
            nc.sync.dma_start(x_rows[:], person_x.rearrange("(b p) k -> p b k", p=P))
            nc.sync.dma_start(wp1_sb[:], wp1)
            nc.sync.dma_start(wp2_sb[:], wp2.rearrange("(a p) d -> p a d", p=P))
            nc.scalar.dma_start(bp1_sb[:], bp1.rearrange("(a p) o -> p (a o)", p=P))
            nc.sync.dma_start(bp2_sb[:], bp2)
            nc.sync.dma_start(t_all[:, 0:CH], t_row[0:CH].partition_broadcast(P))
            nc.sync.dma_start(wt2_sb[:], wt2.rearrange("(p a) d -> p a d", p=P))
            nc.sync.dma_start(wf1_p_sb[:], wf1_p)
        nc.sync.dma_start(offsets[:], offs)
        with nc.allow_non_contiguous_dma(reason="biases: one float32 to a partition and block"):
            nc.sync.dma_start(bt2_sb[:], bt2)
            nc.sync.dma_start(wf1_t_sb[:], wf1_t)
            nc.sync.dma_start(bias_f1_sb[:], bias_f1.rearrange("(a p) o -> p (a o)", p=P))
            nc.sync.dma_start(t_all[:, CH : 2 * CH], t_row[CH : 2 * CH].partition_broadcast(P))
            nc.sync.dma_start(wf2_sb[:], wf2.rearrange("(a p) r -> p a r", p=P))
            nc.sync.dma_start(bias_f2_sb[:], bias_f2.rearrange("(a p) o -> p (a o)", p=P))
        nc.sync.dma_start(state_sb[:, rest], state[:, rest])
        nc.sync.dma_start(t_all[:, 2 * CH : N], t_row[2 * CH : N].partition_broadcast(P))

        warm = held.tile([P, 1], F32, name="warm")
        nc.vector.memset(warm[:], 0.0)
        nc.scalar.activation(warm[:], warm[:], RELU)

        x_t = takeover.tile([P, S], BF16, name="x_t", tag="x_t_then_u")
        a_sb = held.tile([P, HP // P, S], BF16, name="a_sb")
        pe_sb = held.tile([P, S], BF16, name="pe_sb")
        te_sb = held.tile([P, N], BF16, name="te_sb")

        def time_hidden(c):
            cols = slice(c * CH, (c + 1) * CH)
            u_sb = takeover.tile([P, HT // P, CH], BF16, name="u_sb", tag="x_t_then_u")
            for a in range(HT // P):
                nc.scalar.activation(
                    u_sb[:, a, :], t_all[:, cols], RELU, bias=bt1_sb[:, a : a + 1], scale=wt1_sb[:, a : a + 1]
                )
            return u_sb

        def time_encoding(c, u_sb):
            cols = slice(c * CH, (c + 1) * CH)
            te_ps = psum.tile([P, CH], F32, name="te_ps", tag="bank")
            for a in range(HT // P):
                nc.tensor.matmul(
                    te_ps[:], wt2_sb[:, a, :], u_sb[:, a, :], start=(a == 0), stop=(a == HT // P - 1)
                )
            leave_psum(1, te_sb[:, cols], te_ps[:], bt2_sb[:, 0:1], relu=False)

        def open_first_layer(c):
            cols = slice(c * CH, (c + 1) * CH)
            h_ps = [psum.tile([P, CH], F32, name="h_ps%d" % m, tag="h_bank") for m in range(F1 // P)]
            for m in range(F1 // P):
                nc.tensor.matmul(h_ps[m][:], wf1_s_sb[:, m * P : (m + 1) * P], state_sb[:, cols], start=True, stop=False)
            return h_ps

        def time_product(c, h_ps, closes):
            cols = slice(c * CH, (c + 1) * CH)
            for m in range(F1 // P):
                nc.tensor.matmul(h_ps[m][:], wf1_t_sb[:, m * P : (m + 1) * P], te_sb[:, cols], start=False, stop=closes)

        def look_up(c, h_ps, closes):
            picked = pe_sb[:].indirect(offsets[:, c * (CH // 16) : (c + 1) * (CH // 16)])
            for m in range(F1 // P):
                nc.tensor.matmul(h_ps[m][:], wf1_p_sb[:, m * P : (m + 1) * P], picked, start=False, stop=closes)

        for half in range(S // CH):
            x_t_ps = psum.tile([P, CH], BF16, name="x_t_ps", tag="bank")
            for q in range(CH // P):
                nc.tensor.transpose(x_t_ps[:, q * P : (q + 1) * P], x_rows[:, half * (CH // P) + q, :], identity[:])
            nc.vector.tensor_copy(x_t[:, half * CH : (half + 1) * CH], x_t_ps[:])
        h_ps = open_first_layer(0)

        for half in range(S // CH):
            cols = slice(half * CH, (half + 1) * CH)
            for m in range(HP // P):
                a_ps = psum.tile([P, CH], F32, name="a_ps", tag="bank")
                nc.tensor.matmul(a_ps[:], wp1_sb[:, m * P : (m + 1) * P], x_t[:, cols], start=True, stop=True)
                bank = half * (HP // P) + m
                leave_psum(1 if bank == S // CH * (HP // P) - 1 else bank + 1, a_sb[:, m, cols], a_ps[:], bp1_sb[:, m : m + 1], relu=True)
        for half in range(S // CH):
            cols = slice(half * CH, (half + 1) * CH)
            pe_ps = psum.tile([P, CH], F32, name="pe_ps", tag="bank")
            for m in range(HP // P):
                nc.tensor.matmul(pe_ps[:], wp2_sb[:, m, :], a_sb[:, m, cols], start=(m == 0), stop=(m == HP // P - 1))
            leave_psum(1, pe_sb[:, cols], pe_ps[:], bp2_sb[:, 0:1], relu=False)
        time_encoding(0, time_hidden(0))

        for c in range(N // CH):
            cols = slice(c * CH, (c + 1) * CH)
            if c + 1 < N // CH:
                u_next = time_hidden(c + 1)
            if c == 0:
                look_up(c, h_ps, closes=False)
                time_product(c, h_ps, closes=True)
            else:
                time_product(c, h_ps, closes=False)
                look_up(c, h_ps, closes=True)
            h_sb = hidden.tile([P, F1 // P, CH], BF16, name="h_sb")
            for m in range(F1 // P):
                leave_psum(1, h_sb[:, m, :], h_ps[m][:], bias_f1_sb[:, m : m + 1], relu=True)
            if c + 1 < N // CH:
                time_encoding(c + 1, u_next)
                h_ps = open_first_layer(c + 1)
            for r in range(F2 // P):
                last_block = c == N // CH - 1 and r == F2 // P - 1
                width = CH // 4 if last_block else CH
                for piece in range(CH // width):
                    lo = piece * width
                    o_ps = psum.tile([P, width], F32, name="o_ps", tag="bank")
                    for m in range(F1 // P):
                        nc.tensor.matmul(
                            o_ps[:], wf2_sb[:, m, r * P : (r + 1) * P], h_sb[:, m, lo : lo + width],
                            start=(m == 0), stop=(m == F1 // P - 1),
                        )
                    o_sb = staged.tile([P, width], F32, name="o_sb")
                    leave_psum(r + piece, o_sb[:], o_ps[:], bias_f2_sb[:, r : r + 1], relu=True)
                    rows = out[r * P : (r + 1) * P, :]
                    first = c * CH + lo
                    if last_block:
                        store_queue = nc.scalar if (r + piece) % 2 == 0 else nc.sync
                        store_queue.dma_start(rows[:, first : first + width], o_sb[:])
                    else:
                        nc.sync.dma_start(rows[:, first : first + CH // 2], o_sb[:, 0 : CH // 2])
                        nc.scalar.dma_start(rows[:, first + CH // 2 : first + CH], o_sb[:, CH // 2 : CH])
